import numpy as np
import ml_dtypes


def mxq(x, axis, fmt="e4m3"):
    dtype, down = {"e4m3": (ml_dtypes.float8_e4m3fn, 7), "e5m2": (ml_dtypes.float8_e5m2, 14)}[fmt]
    v = np.moveaxis(np.asarray(x, np.float32).astype(ml_dtypes.bfloat16).astype(np.float64), axis, -1)
    blocks = v.reshape(v.shape[:-1] + (-1, 32))
    amax = np.abs(blocks).max(-1, keepdims=True)
    byte = np.maximum(np.where(amax > 0, np.frexp(amax)[1] - 1 + 127, 0) - down, 1)
    scale = np.exp2(byte - 127.0)
    codes = (blocks / scale).astype(np.float32).astype(dtype).astype(np.float64)
    return np.moveaxis((codes * scale).reshape(v.shape), -1, axis)


WIDE = False


def mx_kscale(k):
    if not WIDE:
        return np.ones(k)
    levels = np.array([10, -10, 5, -5, 0])
    a = np.random.permutation(np.resize(levels, k // 512 * 4)).reshape(k // 512, 4)
    idx = np.arange(k)
    return np.exp2(a[idx // 512, idx % 128 // 32])


BF16 = ml_dtypes.bfloat16


def bf(x):
    return np.asarray(x, np.float32).astype(BF16)


def f64(x):
    return np.asarray(x).astype(np.float64)


B, C, H, W, DM, GH = 6, 1024, 16, 16, 128, 1024
OFFSETS = [(-4, -4), (-4, -1), (-4, 2), (-3, 4), (-2, -3), (2, 3), (3, -2), (4, 4)]
N = len(OFFSETS)


def setup_inputs():
    s = mx_kscale(C)
    e = np.exp(0.7 * np.random.standard_normal((N, B)))
    return {'x': bf(np.random.standard_normal((B, C, H, W)) * s[None, :, None, None]),
            'mw': bf(np.random.standard_normal((C, C)) * 2.0 / np.sqrt(C) / s[None, :]),
            'mb': bf(np.random.standard_normal(C) * 0.3),
            'attn_w': bf(e / e.sum(0, keepdims=True))}


def reference(x, mw, mb, attn_w):
    xq = mxq(f64(x).reshape(B, C, H * W), 1, 'e4m3')
    m = (mxq(f64(mw), 1, 'e4m3') @ xq).reshape(B, C, H, W) + f64(mb)[None, :, None, None]
    wts = f64(attn_w)
    agg = np.zeros_like(m)
    for i, (dy, dx) in enumerate(OFFSETS):
        agg = agg + np.roll(m, (dy, dx), axis=(2, 3)) * wts[i][:, None, None, None]
    return agg

@@ -1,0 +1,168 @@
+from contextlib import ExitStack
+
+from concourse import mybir
+from concourse.masks import make_identity
+
+F32 = mybir.dt.float32
+BF16 = mybir.dt.bfloat16
+U32 = mybir.dt.uint32
+U8 = mybir.dt.uint8
+FP8X4 = mybir.dt.float8_e4m3fn_x4
+ACT = mybir.ActivationFunctionType
+ALU = mybir.AluOpType
+
+P = 128
+PACK = 4
+K_PASS = P * PACK
+
+B, C, H, W = 6, 1024, 16, 16
+PIX = H * W
+PASSES = C // K_PASS
+D_TILES = C // P
+OFFSETS = [(-4, -4), (-4, -1), (-4, 2), (-3, 4), (-2, -3), (2, 3), (3, -2), (4, 4)]
+TERMS = len(OFFSETS)
+REACH = 4
+RING_ROWS = H + 2 * REACH
+GROUP = 4
+GROUPS = D_TILES // GROUP
+
+FLOPS = 2 * B * C * C * PIX + 2 * TERMS * B * C * PIX
+
+
+def tile_graphaugmentation_pa_kernel(tc, x, mw, mb, attn_w, out):
+    nc = tc.nc
+    with ExitStack() as stack:
+        const = stack.enter_context(tc.tile_pool(name="const", bufs=1))
+        keep = stack.enter_context(tc.tile_pool(name="keep", bufs=1))
+        stage = stack.enter_context(tc.tile_pool(name="stage", bufs=2))
+        work = stack.enter_context(tc.tile_pool(name="work", bufs=4))
+        psum_t = stack.enter_context(tc.psum_pool(name="psum_t", bufs=2))
+        psum_m = stack.enter_context(tc.psum_pool(name="psum_m", bufs=6))
+
+        x_raw = [keep.tile([P, PASSES * PACK * PIX], BF16, name="x_raw%d" % b) for b in range(B)]
+        mw_raw = keep.tile([P, D_TILES, C], BF16)
+
+        def load_x(b):
+            nc.sync.dma_start(
+                out=x_raw[b][:].rearrange("q (s r) -> q s r", s=PASSES * 2),
+                in_=x[b].rearrange("(s q e) h w -> q s (e h w)", q=P, e=2),
+            )
+
+        w_bf = const.tile([P, TERMS * B], BF16)
+        nc.scalar.dma_start(out=w_bf[:], in_=attn_w.rearrange("i b -> (i b)").partition_broadcast(P))
+        mb_rows = const.tile([P, P], BF16)
+        nc.vector.memset(mb_rows[:], 0.0)
+        nc.scalar.dma_start(out=mb_rows[0:D_TILES, :], in_=mb.rearrange("(t p) -> t p", p=P))
+
+        load_x(0)
+        for pair in range(D_TILES // 2):
+            nc.sync.dma_start(
+                out=mw_raw[:, 2 * pair : 2 * pair + 2, :],
+                in_=mw[2 * pair * P : (2 * pair + 2) * P, :].rearrange("(t p) c -> p t c", p=P),
+            )
+        for b in range(1, B):
+            load_x(b)
+
+        ident = const.tile([P, P], F32)
+        make_identity(nc, ident[:])
+        w_f32 = const.tile([P, TERMS * B], F32)
+        nc.vector.tensor_copy(out=w_f32[:], in_=w_bf[:])
+        mb_rows_f32 = const.tile([P, P], F32)
+        nc.vector.tensor_copy(out=mb_rows_f32[:], in_=mb_rows[:])
+        mb_t = psum_t.tile([P, 4 * P], F32, tag="wT")
+        nc.tensor.transpose(mb_t[:, 0:P], mb_rows_f32[:], ident[:])
+        mb_sb = const.tile([P, D_TILES], F32)
+        nc.vector.tensor_copy(out=mb_sb[:], in_=mb_t[:, 0:D_TILES])
+
+        mw_codes = keep.tile([P, D_TILES, PASSES * P], U32, align_bytes=64)
+        mw_scales = keep.tile([P, D_TILES, PASSES * P], U8, align_bytes=64)
+        for t in range(D_TILES):
+            words = mw_raw[:, t, :].bitcast(F32)
+            wT = psum_t.tile([P, 4 * P], F32, tag="wT")
+            for s in range(PASSES * 2):
+                nc.tensor.transpose(wT[:, s * P : (s + 1) * P], words[:, s * P : (s + 1) * P], ident[:])
+            mw_grp = stage.tile([P, PASSES * P * PACK], BF16, align_bytes=64)
+            nc.scalar.copy(
+                out=mw_grp[:].bitcast(F32).rearrange("q (g d u) -> q g d u", g=PASSES, u=2),
+                in_=wT[:].rearrange("q (g u d) -> q g d u", g=PASSES, u=2),
+            )
+            nc.vector.quantize_mx(
+                out=mw_codes[:, t, :].bitcast(FP8X4), scales=mw_scales[:, t, :], in_=mw_grp[:]
+            )
+
+        x_codes = [keep.tile([P, PASSES * PIX], U32, name="x_codes%d" % b, align_bytes=64) for b in range(B)]
+        x_scales = [keep.tile([P, PASSES * PIX], U8, name="x_scales%d" % b, align_bytes=64) for b in range(B)]
+
+        def quantise_x(b):
+            x_grp = stage.tile([P, PASSES * PIX * PACK], BF16, align_bytes=64)
+            for g in range(PASSES):
+                half = slice(g * PIX * PACK, (g + 1) * PIX * PACK)
+                nc.scalar.copy(
+                    out=x_grp[:, half].rearrange("q (c i t) -> q c t i", i=4, t=PACK),
+                    in_=x_raw[b][:, half].rearrange("q (t c i) -> q c t i", i=4, t=PACK),
+                )
+            nc.vector.quantize_mx(out=x_codes[b][:].bitcast(FP8X4), scales=x_scales[b][:], in_=x_grp[:])
+
+        bank_parts = [(0, PIX // 2, PIX // 2), (PIX // 2, 0, PIX), (PIX // 2 + PIX, 0, PIX // 2)]
+
+        for b in range(B):
+            quantise_x(b)
+            rings, sums = [], []
+            for grp in range(GROUPS):
+                ring = work.tile([P, RING_ROWS, GROUP, 2 * W], F32, name="ring")
+                for j in range(GROUP):
+                    t = grp * GROUP + j
+                    bank = psum_m.tile([P, 2 * PIX], F32, name="bank")
+                    for at, first, n in bank_parts:
+                        for g in range(PASSES):
+                            cols = slice(g * PIX + first, g * PIX + first + n)
+                            nc.tensor.matmul_mx(
+                                out=bank[:, at : at + n],
+                                lhsT=mw_codes[:, t, g * P : (g + 1) * P].bitcast(FP8X4),
+                                lhsT_scale=mw_scales[:, t, g * P : (g + 1) * P],
+                                rhs=x_codes[b][:, cols].bitcast(FP8X4),
+                                rhs_scale=x_scales[b][:, cols],
+                                start=(g == 0),
+                                stop=(g == PASSES - 1),
+                            )
+                    rows = bank[:, (H // 2 - REACH) * W : (H // 2 - REACH + RING_ROWS) * W]
+                    nc.scalar.activation(
+                        out=ring[:, :, j, :].rearrange("p r (c w) -> p r c w", c=2),
+                        in_=rows.rearrange("p (r w) -> p r w", w=W).unsqueeze(2).to_broadcast([P, RING_ROWS, 2, W]),
+                        func=ACT.Identity,
+                        bias=mb_sb[:, t : t + 1],
+                        scale=1.0,
+                    )
+                rings.append(ring)
+
+            def shifted(ring, i):
+                dy, dx = OFFSETS[i]
+                return ring[:, REACH - dy : REACH - dy + H, :, (-dx) % W : (-dx) % W + W]
+
+            def weight(i):
+                return w_f32[:, i * B + b : i * B + b + 1]
+
+            for grp in range(GROUPS):
+                acc = work.tile([P, H, GROUP, W], F32, name="acc")
+                nc.scalar.activation(out=acc[:], in_=shifted(rings[grp], 0), func=ACT.Copy, scale=weight(0))
+                sums.append(acc)
+            for i in range(1, TERMS - 1):
+                for grp in range(GROUPS):
+                    nc.vector.scalar_tensor_tensor(
+                        out=sums[grp][:], in0=shifted(rings[grp], i), scalar=weight(i), in1=sums[grp][:],
+                        op0=ALU.mult, op1=ALU.add,
+                    )
+            for grp in range(GROUPS):
+                res = work.tile([P, GROUP, PIX], F32, name="res")
+                for j in range(GROUP):
+                    nc.vector.scalar_tensor_tensor(
+                        out=res[:, j, :].rearrange("p (h w) -> p h w", w=W),
+                        in0=shifted(rings[grp], TERMS - 1)[:, :, j, :],
+                        scalar=weight(TERMS - 1),
+                        in1=sums[grp][:, :, j, :],
+                        op0=ALU.mult, op1=ALU.add,
+                    )
+                nc.sync.dma_start(
+                    out=out[b, grp * GROUP * P : (grp + 1) * GROUP * P].rearrange("(j p) h w -> p j (h w)", p=P),
+                    in_=res[:],
+                )

@@ -14,9 +14,11 @@ ALU = mybir.AluOpType
 P = 128
 PACK = 4
 K_PASS = P * PACK
+BANK = 512
 
 B, C, H, W = 6, 1024, 16, 16
 PIX = H * W
+PIX_TILES = PIX // P
 PASSES = C // K_PASS
 D_TILES = C // P
 OFFSETS = [(-4, -4), (-4, -1), (-4, 2), (-3, 4), (-2, -3), (2, 3), (3, -2), (4, 4)]
@@ -25,8 +27,13 @@ REACH = 4
 RING_ROWS = H + 2 * REACH
 GROUP = 4
 GROUPS = D_TILES // GROUP
+AHEAD = 2
 
 FLOPS = 2 * B * C * C * PIX + 2 * TERMS * B * C * PIX
+
+
+def by_matrix(b):
+    return b % 3 == 2
 
 
 def tile_graphaugmentation_pa_kernel(tc, x, mw, mb, attn_w, out):
@@ -67,18 +74,69 @@ def tile_graphaugmentation_pa_kernel(tc, x, mw, mb, attn_w, out):
         make_identity(nc, ident[:])
         w_f32 = const.tile([P, TERMS * B], F32)
         nc.vector.tensor_copy(out=w_f32[:], in_=w_bf[:])
+
+        def weight(i, b):
+            return w_f32[:, i * B + b : i * B + b + 1]
+
+        def shifted(ring, i):
+            dy, dx = OFFSETS[i]
+            return ring[:, REACH - dy : REACH - dy + H, :, (-dx) % W : (-dx) % W + W]
+
+        def first_term(ring, n, b):
+            acc = work.tile([P, H, n, W], F32, name="acc%d" % n)
+            nc.scalar.activation(out=acc[:], in_=shifted(ring, 0), func=ACT.Copy, scale=weight(0, b))
+            return acc
+
+        def other_terms(chains):
+            for i in range(1, TERMS - 1):
+                for ring, n, b, acc, res in chains:
+                    nc.vector.scalar_tensor_tensor(
+                        out=acc[:], in0=shifted(ring, i), scalar=weight(i, b), in1=acc[:], op0=ALU.mult, op1=ALU.add
+                    )
+            for ring, n, b, acc, res in chains:
+                for j in range(n):
+                    nc.vector.scalar_tensor_tensor(
+                        out=res[:, j, :].rearrange("p (h w) -> p h w", w=W),
+                        in0=shifted(ring, TERMS - 1)[:, :, j, :],
+                        scalar=weight(TERMS - 1, b),
+                        in1=acc[:, :, j, :],
+                        op0=ALU.mult,
+                        op1=ALU.add,
+                    )
+
+        eye = const.tile([P, PIX_TILES, PIX], F32)
+        nc.gpsimd.memset(eye[:], 0.0)
+        eye_ring = const.tile([P, RING_ROWS, PIX_TILES, 2 * W], F32)
+        for j in range(PIX_TILES):
+            nc.vector.tensor_copy(out=eye[:, j, j * P : (j + 1) * P], in_=ident[:])
+            for ring_row, image_row, n in [(0, H - REACH, REACH), (REACH, 0, H), (REACH + H, 0, REACH)]:
+                nc.vector.tensor_copy(
+                    out=eye_ring[:, ring_row : ring_row + n, j, :].rearrange("p r (c w) -> p r c w", c=2),
+                    in_=eye[:, j, image_row * W : (image_row + n) * W]
+                    .rearrange("p (r w) -> p r w", w=W)
+                    .unsqueeze(2)
+                    .to_broadcast([P, n, 2, W]),
+                )
+        matrix = dict((b, const.tile([P, PIX_TILES, PIX], F32, name="matrix%d" % b)) for b in range(B) if by_matrix(b))
+        other_terms([(eye_ring, PIX_TILES, b, first_term(eye_ring, PIX_TILES, b), matrix[b]) for b in matrix])
+
         mb_rows_f32 = const.tile([P, P], F32)
         nc.vector.tensor_copy(out=mb_rows_f32[:], in_=mb_rows[:])
-        mb_t = psum_t.tile([P, 4 * P], F32, tag="wT")
+        mb_t = psum_t.tile([P, BANK], F32, tag="wT")
         nc.tensor.transpose(mb_t[:, 0:P], mb_rows_f32[:], ident[:])
         mb_sb = const.tile([P, D_TILES], F32)
         nc.vector.tensor_copy(out=mb_sb[:], in_=mb_t[:, 0:D_TILES])
+        w_sum = const.tile([P, B], F32)
+        nc.vector.reduce_sum(out=w_sum[:], in_=w_f32[:].rearrange("p (i b) -> p b i", b=B), axis=mybir.AxisListType.X)
+        mb_w = dict((b, const.tile([P, D_TILES], F32, name="mb_w%d" % b)) for b in matrix)
+        for b in matrix:
+            nc.vector.tensor_scalar_mul(out=mb_w[b][:], in0=mb_sb[:], scalar1=w_sum[:, b : b + 1])
 
-        mw_codes = keep.tile([P, D_TILES, PASSES * P], U32, align_bytes=64)
-        mw_scales = keep.tile([P, D_TILES, PASSES * P], U8, align_bytes=64)
+        mw_codes = keep.tile([P, PASSES, C], U32, align_bytes=64)
+        mw_scales = keep.tile([P, PASSES, C], U8, align_bytes=64)
         for t in range(D_TILES):
             words = mw_raw[:, t, :].bitcast(F32)
-            wT = psum_t.tile([P, 4 * P], F32, tag="wT")
+            wT = psum_t.tile([P, BANK], F32, tag="wT")
             for s in range(PASSES * 2):
                 nc.tensor.transpose(wT[:, s * P : (s + 1) * P], words[:, s * P : (s + 1) * P], ident[:])
             mw_grp = stage.tile([P, PASSES * P * PACK], BF16, align_bytes=64)
@@ -86,45 +144,56 @@ def tile_graphaugmentation_pa_kernel(tc, x, mw, mb, attn_w, out):
                 out=mw_grp[:].bitcast(F32).rearrange("q (g d u) -> q g d u", g=PASSES, u=2),
                 in_=wT[:].rearrange("q (g u d) -> q g d u", g=PASSES, u=2),
             )
-            nc.vector.quantize_mx(
-                out=mw_codes[:, t, :].bitcast(FP8X4), scales=mw_scales[:, t, :], in_=mw_grp[:]
-            )
+            for g in range(PASSES):
+                nc.vector.quantize_mx(
+                    out=mw_codes[:, g, t * P : (t + 1) * P].bitcast(FP8X4),
+                    scales=mw_scales[:, g, t * P : (t + 1) * P],
+                    in_=mw_grp[:, g * P * PACK : (g + 1) * P * PACK],
+                )
 
-        x_codes = [keep.tile([P, PASSES * PIX], U32, name="x_codes%d" % b, align_bytes=64) for b in range(B)]
-        x_scales = [keep.tile([P, PASSES * PIX], U8, name="x_scales%d" % b, align_bytes=64) for b in range(B)]
+        x_codes = [keep.tile([P, PASSES, PIX], U32, name="x_codes%d" % b, align_bytes=64) for b in range(B)]
+        x_scales = [keep.tile([P, PASSES, PIX], U8, name="x_scales%d" % b, align_bytes=64) for b in range(B)]
 
         def quantise_x(b):
+            regroup = nc.vector.tensor_copy if b < AHEAD else nc.scalar.copy
             x_grp = stage.tile([P, PASSES * PIX * PACK], BF16, align_bytes=64)
             for g in range(PASSES):
                 half = slice(g * PIX * PACK, (g + 1) * PIX * PACK)
-                nc.scalar.copy(
+                regroup(
                     out=x_grp[:, half].rearrange("q (c i t) -> q c t i", i=4, t=PACK),
                     in_=x_raw[b][:, half].rearrange("q (t c i) -> q c t i", i=4, t=PACK),
                 )
-            nc.vector.quantize_mx(out=x_codes[b][:].bitcast(FP8X4), scales=x_scales[b][:], in_=x_grp[:])
+            nc.vector.quantize_mx(
+                out=x_codes[b][:].rearrange("q g c -> q (g c)").bitcast(FP8X4),
+                scales=x_scales[b][:].rearrange("q g c -> q (g c)"),
+                in_=x_grp[:],
+            )
 
-        bank_parts = [(0, PIX // 2, PIX // 2), (PIX // 2, 0, PIX), (PIX // 2 + PIX, 0, PIX // 2)]
+        def mx_group(acc, b, pixels, channels, channels_stationary):
+            for g in range(PASSES):
+                mw_side = (mw_codes[:, g, channels].bitcast(FP8X4), mw_scales[:, g, channels])
+                x_side = (x_codes[b][:, g, pixels].bitcast(FP8X4), x_scales[b][:, g, pixels])
+                still, moving = (mw_side, x_side) if channels_stationary else (x_side, mw_side)
+                nc.tensor.matmul_mx(
+                    out=acc, lhsT=still[0], lhsT_scale=still[1], rhs=moving[0], rhs_scale=moving[1],
+                    start=(g == 0), stop=(g == PASSES - 1),
+                )
 
-        for b in range(B):
-            quantise_x(b)
-            rings, sums = [], []
+        def store(b, grp, res):
+            nc.sync.dma_start(
+                out=out[b, grp * GROUP * P : (grp + 1) * GROUP * P].rearrange("(j p) h w -> p j (h w)", p=P),
+                in_=res[:],
+            )
+
+        def messages(b):
+            chains = []
             for grp in range(GROUPS):
-                ring = work.tile([P, RING_ROWS, GROUP, 2 * W], F32, name="ring")
+                ring = work.tile([P, RING_ROWS, GROUP, 2 * W], F32, name="ring", bufs=6)
                 for j in range(GROUP):
                     t = grp * GROUP + j
-                    bank = psum_m.tile([P, 2 * PIX], F32, name="bank")
-                    for at, first, n in bank_parts:
-                        for g in range(PASSES):
-                            cols = slice(g * PIX + first, g * PIX + first + n)
-                            nc.tensor.matmul_mx(
-                                out=bank[:, at : at + n],
-                                lhsT=mw_codes[:, t, g * P : (g + 1) * P].bitcast(FP8X4),
-                                lhsT_scale=mw_scales[:, t, g * P : (g + 1) * P],
-                                rhs=x_codes[b][:, cols].bitcast(FP8X4),
-                                rhs_scale=x_scales[b][:, cols],
-                                start=(g == 0),
-                                stop=(g == PASSES - 1),
-                            )
+                    bank = psum_m.tile([P, BANK], F32, name="bank")
+                    for at, first, n in [(0, PIX // 2, PIX // 2), (PIX // 2, 0, PIX), (PIX // 2 + PIX, 0, PIX // 2)]:
+                        mx_group(bank[:, at : at + n], b, slice(first, first + n), slice(t * P, (t + 1) * P), True)
                     rows = bank[:, (H // 2 - REACH) * W : (H // 2 - REACH + RING_ROWS) * W]
                     nc.scalar.activation(
                         out=ring[:, :, j, :].rearrange("p r (c w) -> p r c w", c=2),
@@ -133,36 +202,57 @@ def tile_graphaugmentation_pa_kernel(tc, x, mw, mb, attn_w, out):
                         bias=mb_sb[:, t : t + 1],
                         scale=1.0,
                     )
-                rings.append(ring)
+                chains.append((ring, GROUP, b, first_term(ring, GROUP, b)))
+            return chains
 
-            def shifted(ring, i):
-                dy, dx = OFFSETS[i]
-                return ring[:, REACH - dy : REACH - dy + H, :, (-dx) % W : (-dx) % W + W]
-
-            def weight(i):
-                return w_f32[:, i * B + b : i * B + b + 1]
-
-            for grp in range(GROUPS):
-                acc = work.tile([P, H, GROUP, W], F32, name="acc")
-                nc.scalar.activation(out=acc[:], in_=shifted(rings[grp], 0), func=ACT.Copy, scale=weight(0))
-                sums.append(acc)
-            for i in range(1, TERMS - 1):
-                for grp in range(GROUPS):
-                    nc.vector.scalar_tensor_tensor(
-                        out=sums[grp][:], in0=shifted(rings[grp], i), scalar=weight(i), in1=sums[grp][:],
-                        op0=ALU.mult, op1=ALU.add,
-                    )
+        def through_matrix(b):
+            m_t = work.tile([P, PIX_TILES, C], F32, name="m_t", bufs=2)
+            for j in range(PIX_TILES):
+                for n in range(C // BANK):
+                    bank = psum_m.tile([P, BANK], F32, name="bank")
+                    mx_group(bank[:], b, slice(j * P, (j + 1) * P), slice(n * BANK, (n + 1) * BANK), False)
+                    nc.scalar.copy(out=m_t[:, j, n * BANK : (n + 1) * BANK], in_=bank[:])
             for grp in range(GROUPS):
                 res = work.tile([P, GROUP, PIX], F32, name="res")
-                for j in range(GROUP):
-                    nc.vector.scalar_tensor_tensor(
-                        out=res[:, j, :].rearrange("p (h w) -> p h w", w=W),
-                        in0=shifted(rings[grp], TERMS - 1)[:, :, j, :],
-                        scalar=weight(TERMS - 1),
-                        in1=sums[grp][:, :, j, :],
-                        op0=ALU.mult, op1=ALU.add,
-                    )
-                nc.sync.dma_start(
-                    out=out[b, grp * GROUP * P : (grp + 1) * GROUP * P].rearrange("(j p) h w -> p j (h w)", p=P),
-                    in_=res[:],
-                )
+                for pair in range(GROUP // 2):
+                    bank = psum_m.tile([P, BANK], F32, name="bank")
+                    for k in range(2):
+                        t = grp * GROUP + 2 * pair + k
+                        for j in range(PIX_TILES):
+                            nc.tensor.matmul(
+                                out=bank[:, k * PIX : (k + 1) * PIX],
+                                lhsT=m_t[:, j, t * P : (t + 1) * P],
+                                rhs=matrix[b][:, j, :],
+                                start=(j == 0),
+                                stop=(j == PIX_TILES - 1),
+                            )
+                    for k in range(2):
+                        t = grp * GROUP + 2 * pair + k
+                        nc.scalar.activation(
+                            out=res[:, 2 * pair + k, :],
+                            in_=bank[:, k * PIX : (k + 1) * PIX],
+                            func=ACT.Identity,
+                            bias=mb_w[b][:, t : t + 1],
+                            scale=1.0,
+                        )
+                store(b, grp, res)
+
+        def multiply(b):
+            if by_matrix(b):
+                through_matrix(b)
+                return []
+            return messages(b)
+
+        for b in range(AHEAD):
+            quantise_x(b)
+        ahead = multiply(0)
+        for b in range(B):
+            chains = ahead
+            if b + AHEAD < B:
+                quantise_x(b + AHEAD)
+            if b + 1 < B:
+                ahead = multiply(b + 1)
+            results = [work.tile([P, GROUP, PIX], F32, name="res") for chain in chains]
+            other_terms([chain + (res,) for chain, res in zip(chains, results)])
+            for grp, res in enumerate(results):
+                store(b, grp, res)

@@ -18,13 +18,12 @@ BANK = 512
 
 B, C, H, W = 6, 1024, 16, 16
 PIX = H * W
-PIX_TILES = PIX // P
+HALF_ROWS = H // 2
 PASSES = C // K_PASS
 D_TILES = C // P
 OFFSETS = [(-4, -4), (-4, -1), (-4, 2), (-3, 4), (-2, -3), (2, 3), (3, -2), (4, 4)]
 TERMS = len(OFFSETS)
 REACH = 4
-RING_ROWS = H + 2 * REACH
 GROUP = 4
 GROUPS = D_TILES // GROUP
 AHEAD = 2
@@ -33,18 +32,18 @@ FLOPS = 2 * B * C * C * PIX + 2 * TERMS * B * C * PIX
 
 
 def by_matrix(b):
-    return b % 3 == 2
+    return b % 3 != 0
 
 
 def tile_graphaugmentation_pa_kernel(tc, x, mw, mb, attn_w, out):
     nc = tc.nc
+    matrix_images = [b for b in range(B) if by_matrix(b)]
     with ExitStack() as stack:
         const = stack.enter_context(tc.tile_pool(name="const", bufs=1))
         keep = stack.enter_context(tc.tile_pool(name="keep", bufs=1))
         stage = stack.enter_context(tc.tile_pool(name="stage", bufs=2))
         work = stack.enter_context(tc.tile_pool(name="work", bufs=4))
-        psum_t = stack.enter_context(tc.psum_pool(name="psum_t", bufs=2))
-        psum_m = stack.enter_context(tc.psum_pool(name="psum_m", bufs=6))
+        psum = stack.enter_context(tc.psum_pool(name="psum", bufs=8))
 
         x_raw = [keep.tile([P, PASSES * PACK * PIX], BF16, name="x_raw%d" % b) for b in range(B)]
         mw_raw = keep.tile([P, D_TILES, C], BF16)
@@ -78,71 +77,74 @@ def tile_graphaugmentation_pa_kernel(tc, x, mw, mb, attn_w, out):
         def weight(i, b):
             return w_f32[:, i * B + b : i * B + b + 1]
 
-        def shifted(ring, i):
+        def shifted(ring, i, rows):
             dy, dx = OFFSETS[i]
-            return ring[:, REACH - dy : REACH - dy + H, :, (-dx) % W : (-dx) % W + W]
+            return ring[:, REACH - dy : REACH - dy + rows, :, (-dx) % W : (-dx) % W + W]
 
-        def first_term(ring, n, b):
-            acc = work.tile([P, H, n, W], F32, name="acc%d" % n)
-            nc.scalar.activation(out=acc[:], in_=shifted(ring, 0), func=ACT.Copy, scale=weight(0, b))
-            return acc
+        def first_term(ring, rows, n, b):
+            acc = work.tile([P, rows, n, W], F32, name="acc%dx%d" % (rows, n))
+            nc.scalar.activation(out=acc[:], in_=shifted(ring, 0, rows), func=ACT.Copy, scale=weight(0, b))
+            return (ring, rows, n, b, acc)
 
         def other_terms(chains):
             for i in range(1, TERMS - 1):
-                for ring, n, b, acc, res in chains:
+                for ring, rows, n, b, acc, res in chains:
                     nc.vector.scalar_tensor_tensor(
-                        out=acc[:], in0=shifted(ring, i), scalar=weight(i, b), in1=acc[:], op0=ALU.mult, op1=ALU.add
+                        out=acc[:], in0=shifted(ring, i, rows), scalar=weight(i, b), in1=acc[:],
+                        op0=ALU.mult, op1=ALU.add,
                     )
-            for ring, n, b, acc, res in chains:
+            for ring, rows, n, b, acc, res in chains:
                 for j in range(n):
                     nc.vector.scalar_tensor_tensor(
                         out=res[:, j, :].rearrange("p (h w) -> p h w", w=W),
-                        in0=shifted(ring, TERMS - 1)[:, :, j, :],
+                        in0=shifted(ring, TERMS - 1, rows)[:, :, j, :],
                         scalar=weight(TERMS - 1, b),
                         in1=acc[:, :, j, :],
                         op0=ALU.mult,
                         op1=ALU.add,
                     )
 
-        eye = const.tile([P, PIX_TILES, PIX], F32)
-        nc.gpsimd.memset(eye[:], 0.0)
-        eye_ring = const.tile([P, RING_ROWS, PIX_TILES, 2 * W], F32)
-        for j in range(PIX_TILES):
-            nc.vector.tensor_copy(out=eye[:, j, j * P : (j + 1) * P], in_=ident[:])
-            for ring_row, image_row, n in [(0, H - REACH, REACH), (REACH, 0, H), (REACH + H, 0, REACH)]:
-                nc.vector.tensor_copy(
-                    out=eye_ring[:, ring_row : ring_row + n, j, :].rearrange("p r (c w) -> p r c w", c=2),
-                    in_=eye[:, j, image_row * W : (image_row + n) * W]
+        fold_ring = const.tile([P, HALF_ROWS + 2 * REACH, 2, 2 * W], F32)
+        for ring_row, image_row, n, over_the_edge in [
+            (0, HALF_ROWS - REACH, REACH, True),
+            (REACH, 0, HALF_ROWS, False),
+            (REACH + HALF_ROWS, 0, REACH, True),
+        ]:
+            for sign in range(2):
+                nc.vector.tensor_scalar_mul(
+                    out=fold_ring[:, ring_row : ring_row + n, sign, :].rearrange("p r (c w) -> p r c w", c=2),
+                    in0=ident[:, image_row * W : (image_row + n) * W]
                     .rearrange("p (r w) -> p r w", w=W)
                     .unsqueeze(2)
                     .to_broadcast([P, n, 2, W]),
+                    scalar1=(-0.5 if over_the_edge and sign == 1 else 0.5),
                 )
-        matrix = dict((b, const.tile([P, PIX_TILES, PIX], F32, name="matrix%d" % b)) for b in range(B) if by_matrix(b))
-        other_terms([(eye_ring, PIX_TILES, b, first_term(eye_ring, PIX_TILES, b), matrix[b]) for b in matrix])
+        matrix = dict((b, const.tile([P, 2, P], F32, name="matrix%d" % b)) for b in matrix_images)
+        other_terms([first_term(fold_ring, HALF_ROWS, 2, b) + (matrix[b],) for b in matrix_images])
 
         mb_rows_f32 = const.tile([P, P], F32)
         nc.vector.tensor_copy(out=mb_rows_f32[:], in_=mb_rows[:])
-        mb_t = psum_t.tile([P, BANK], F32, tag="wT")
+        mb_t = psum.tile([P, BANK], F32, tag="bank")
         nc.tensor.transpose(mb_t[:, 0:P], mb_rows_f32[:], ident[:])
         mb_sb = const.tile([P, D_TILES], F32)
         nc.vector.tensor_copy(out=mb_sb[:], in_=mb_t[:, 0:D_TILES])
         w_sum = const.tile([P, B], F32)
         nc.vector.reduce_sum(out=w_sum[:], in_=w_f32[:].rearrange("p (i b) -> p b i", b=B), axis=mybir.AxisListType.X)
-        mb_w = dict((b, const.tile([P, D_TILES], F32, name="mb_w%d" % b)) for b in matrix)
-        for b in matrix:
+        mb_w = dict((b, const.tile([P, D_TILES], F32, name="mb_w%d" % b)) for b in matrix_images)
+        for b in matrix_images:
             nc.vector.tensor_scalar_mul(out=mb_w[b][:], in0=mb_sb[:], scalar1=w_sum[:, b : b + 1])
 
         mw_codes = keep.tile([P, PASSES, C], U32, align_bytes=64)
         mw_scales = keep.tile([P, PASSES, C], U8, align_bytes=64)
         for t in range(D_TILES):
             words = mw_raw[:, t, :].bitcast(F32)
-            wT = psum_t.tile([P, BANK], F32, tag="wT")
+            w_t = psum.tile([P, BANK], F32, tag="bank")
             for s in range(PASSES * 2):
-                nc.tensor.transpose(wT[:, s * P : (s + 1) * P], words[:, s * P : (s + 1) * P], ident[:])
+                nc.tensor.transpose(w_t[:, s * P : (s + 1) * P], words[:, s * P : (s + 1) * P], ident[:])
             mw_grp = stage.tile([P, PASSES * P * PACK], BF16, align_bytes=64)
             nc.scalar.copy(
                 out=mw_grp[:].bitcast(F32).rearrange("q (g d u) -> q g d u", g=PASSES, u=2),
-                in_=wT[:].rearrange("q (g u d) -> q g d u", g=PASSES, u=2),
+                in_=w_t[:].rearrange("q (g u d) -> q g d u", g=PASSES, u=2),
             )
             for g in range(PASSES):
                 nc.vector.quantize_mx(
@@ -153,30 +155,56 @@ def tile_graphaugmentation_pa_kernel(tc, x, mw, mb, attn_w, out):
 
         x_codes = [keep.tile([P, PASSES, PIX], U32, name="x_codes%d" % b, align_bytes=64) for b in range(B)]
         x_scales = [keep.tile([P, PASSES, PIX], U8, name="x_scales%d" % b, align_bytes=64) for b in range(B)]
+        minus_codes = dict((b, keep.tile([P, PASSES, P], U32, name="minus_codes%d" % b, align_bytes=64)) for b in matrix_images)
+        minus_scales = dict((b, keep.tile([P, PASSES, P], U8, name="minus_scales%d" % b, align_bytes=64)) for b in matrix_images)
 
         def quantise_x(b):
             regroup = nc.vector.tensor_copy if b < AHEAD else nc.scalar.copy
-            x_grp = stage.tile([P, PASSES * PIX * PACK], BF16, align_bytes=64)
+            rows_of_words = x_raw[b][:].rearrange("q (g t c) -> q g t c", g=PASSES, t=PACK)
+            x_grp = stage.tile([P, PASSES, PIX * PACK], BF16, align_bytes=64)
             for g in range(PASSES):
-                half = slice(g * PIX * PACK, (g + 1) * PIX * PACK)
                 regroup(
-                    out=x_grp[:, half].rearrange("q (c i t) -> q c t i", i=4, t=PACK),
-                    in_=x_raw[b][:, half].rearrange("q (t c i) -> q c t i", i=4, t=PACK),
+                    out=x_grp[:, g, :].rearrange("q (c i t) -> q c t i", i=4, t=PACK),
+                    in_=rows_of_words[:, g, :, :].rearrange("q t (c i) -> q c t i", i=4),
                 )
             nc.vector.quantize_mx(
                 out=x_codes[b][:].rearrange("q g c -> q (g c)").bitcast(FP8X4),
                 scales=x_scales[b][:].rearrange("q g c -> q (g c)"),
-                in_=x_grp[:],
+                in_=x_grp[:].rearrange("q g c -> q (g c)"),
             )
+            if by_matrix(b):
+                minus_grp = stage.tile([P, PASSES, P * PACK], BF16, align_bytes=64)
+                for g in range(PASSES):
+                    nc.scalar.mul(
+                        out=minus_grp[:, g, :].rearrange("q (c i t) -> q c t i", i=4, t=PACK),
+                        in_=rows_of_words[:, g, :, P : 2 * P].rearrange("q t (c i) -> q c t i", i=4),
+                        mul=-1.0,
+                    )
+                nc.vector.quantize_mx(
+                    out=minus_codes[b][:].rearrange("q g c -> q (g c)").bitcast(FP8X4),
+                    scales=minus_scales[b][:].rearrange("q g c -> q (g c)"),
+                    in_=minus_grp[:].rearrange("q g c -> q (g c)"),
+                )
 
-        def mx_group(acc, b, pixels, channels, channels_stationary):
-            for g in range(PASSES):
-                mw_side = (mw_codes[:, g, channels].bitcast(FP8X4), mw_scales[:, g, channels])
-                x_side = (x_codes[b][:, g, pixels].bitcast(FP8X4), x_scales[b][:, g, pixels])
-                still, moving = (mw_side, x_side) if channels_stationary else (x_side, mw_side)
+        def mw_part(g, channels):
+            return (mw_codes[:, g, channels], mw_scales[:, g, channels])
+
+        def x_part(b, g, pixels):
+            return (x_codes[b][:, g, pixels], x_scales[b][:, g, pixels])
+
+        def minus_part(b, g):
+            return (minus_codes[b][:, g, :], minus_scales[b][:, g, :])
+
+        def mx_group(acc, pairs):
+            for k, (still, moving) in enumerate(pairs):
                 nc.tensor.matmul_mx(
-                    out=acc, lhsT=still[0], lhsT_scale=still[1], rhs=moving[0], rhs_scale=moving[1],
-                    start=(g == 0), stop=(g == PASSES - 1),
+                    out=acc,
+                    lhsT=still[0].bitcast(FP8X4),
+                    lhsT_scale=still[1],
+                    rhs=moving[0].bitcast(FP8X4),
+                    rhs_scale=moving[1],
+                    start=(k == 0),
+                    stop=(k == len(pairs) - 1),
                 )
 
         def store(b, grp, res):
@@ -185,74 +213,103 @@ def tile_graphaugmentation_pa_kernel(tc, x, mw, mb, attn_w, out):
                 in_=res[:],
             )
 
-        def messages(b):
+        def multiply_direct(b):
             chains = []
             for grp in range(GROUPS):
-                ring = work.tile([P, RING_ROWS, GROUP, 2 * W], F32, name="ring", bufs=6)
+                ring = work.tile([P, H + 2 * REACH, GROUP, 2 * W], F32, name="ring")
                 for j in range(GROUP):
                     t = grp * GROUP + j
-                    bank = psum_m.tile([P, BANK], F32, name="bank")
+                    channels = slice(t * P, (t + 1) * P)
+                    bank = psum.tile([P, BANK], F32, tag="bank")
                     for at, first, n in [(0, PIX // 2, PIX // 2), (PIX // 2, 0, PIX), (PIX // 2 + PIX, 0, PIX // 2)]:
-                        mx_group(bank[:, at : at + n], b, slice(first, first + n), slice(t * P, (t + 1) * P), True)
-                    rows = bank[:, (H // 2 - REACH) * W : (H // 2 - REACH + RING_ROWS) * W]
+                        mx_group(
+                            bank[:, at : at + n],
+                            [(mw_part(g, channels), x_part(b, g, slice(first, first + n))) for g in range(PASSES)],
+                        )
+                    rows = bank[:, (HALF_ROWS - REACH) * W : (HALF_ROWS + H + REACH) * W]
                     nc.scalar.activation(
                         out=ring[:, :, j, :].rearrange("p r (c w) -> p r c w", c=2),
-                        in_=rows.rearrange("p (r w) -> p r w", w=W).unsqueeze(2).to_broadcast([P, RING_ROWS, 2, W]),
+                        in_=rows.rearrange("p (r w) -> p r w", w=W).unsqueeze(2).to_broadcast([P, H + 2 * REACH, 2, W]),
                         func=ACT.Identity,
                         bias=mb_sb[:, t : t + 1],
                         scale=1.0,
                     )
-                chains.append((ring, GROUP, b, first_term(ring, GROUP, b)))
+                chains.append(first_term(ring, H, GROUP, b))
             return chains
 
-        def through_matrix(b):
-            m_t = work.tile([P, PIX_TILES, C], F32, name="m_t", bufs=2)
-            for j in range(PIX_TILES):
+        def finish_direct(b, chains):
+            results = [work.tile([P, GROUP, PIX], F32, name="res") for chain in chains]
+            other_terms([chain + (res,) for chain, res in zip(chains, results)])
+            for grp, res in enumerate(results):
+                store(b, grp, res)
+
+        def multiply_by_matrix(b):
+            folded = work.tile([P, 2, C], F32, name="folded", bufs=2)
+            for sign in range(2):
                 for n in range(C // BANK):
-                    bank = psum_m.tile([P, BANK], F32, name="bank")
-                    mx_group(bank[:], b, slice(j * P, (j + 1) * P), slice(n * BANK, (n + 1) * BANK), False)
-                    nc.scalar.copy(out=m_t[:, j, n * BANK : (n + 1) * BANK], in_=bank[:])
+                    channels = slice(n * BANK, (n + 1) * BANK)
+                    bank = psum.tile([P, BANK], F32, tag="bank")
+                    lower = [(x_part(b, g, slice(0, P)), mw_part(g, channels)) for g in range(PASSES)]
+                    upper = [
+                        (x_part(b, g, slice(P, 2 * P)) if sign == 0 else minus_part(b, g), mw_part(g, channels))
+                        for g in range(PASSES)
+                    ]
+                    mx_group(bank[:], lower + upper)
+                    nc.scalar.copy(out=folded[:, sign, channels], in_=bank[:])
+            parts = []
             for grp in range(GROUPS):
-                res = work.tile([P, GROUP, PIX], F32, name="res")
-                for pair in range(GROUP // 2):
-                    bank = psum_m.tile([P, BANK], F32, name="bank")
-                    for k in range(2):
-                        t = grp * GROUP + 2 * pair + k
-                        for j in range(PIX_TILES):
-                            nc.tensor.matmul(
-                                out=bank[:, k * PIX : (k + 1) * PIX],
-                                lhsT=m_t[:, j, t * P : (t + 1) * P],
-                                rhs=matrix[b][:, j, :],
-                                start=(j == 0),
-                                stop=(j == PIX_TILES - 1),
-                            )
-                    for k in range(2):
-                        t = grp * GROUP + 2 * pair + k
-                        nc.scalar.activation(
-                            out=res[:, 2 * pair + k, :],
-                            in_=bank[:, k * PIX : (k + 1) * PIX],
-                            func=ACT.Identity,
-                            bias=mb_w[b][:, t : t + 1],
-                            scale=1.0,
+                bank_u = psum.tile([P, BANK], F32, tag="bank")
+                bank_v = psum.tile([P, BANK], F32, tag="bank")
+                for sign, bank in enumerate((bank_u, bank_v)):
+                    for j in range(GROUP):
+                        t = grp * GROUP + j
+                        nc.tensor.matmul(
+                            out=bank[:, j * P : (j + 1) * P],
+                            lhsT=folded[:, sign, t * P : (t + 1) * P],
+                            rhs=matrix[b][:, sign, :],
+                            start=True,
+                            stop=True,
                         )
+                u_sb = work.tile([P, GROUP, P], F32, name="u_sb")
+                for j in range(GROUP):
+                    t = grp * GROUP + j
+                    nc.scalar.activation(
+                        out=u_sb[:, j, :],
+                        in_=bank_u[:, j * P : (j + 1) * P],
+                        func=ACT.Identity,
+                        bias=mb_w[b][:, t : t + 1],
+                        scale=1.0,
+                    )
+                parts.append((u_sb, bank_v))
+            return parts
+
+        def finish_by_matrix(b, parts):
+            for grp, (u_sb, bank_v) in enumerate(parts):
+                res = work.tile([P, GROUP, PIX], F32, name="res")
+                for half, sign in enumerate((1.0, -1.0)):
+                    nc.vector.scalar_tensor_tensor(
+                        out=res[:, :, half * P : (half + 1) * P],
+                        in0=bank_v[:].rearrange("p (j c) -> p j c", j=GROUP),
+                        scalar=sign,
+                        in1=u_sb[:],
+                        op0=ALU.mult,
+                        op1=ALU.add,
+                    )
                 store(b, grp, res)
 
         def multiply(b):
-            if by_matrix(b):
-                through_matrix(b)
-                return []
-            return messages(b)
+            return multiply_by_matrix(b) if by_matrix(b) else multiply_direct(b)
 
         for b in range(AHEAD):
             quantise_x(b)
         ahead = multiply(0)
         for b in range(B):
-            chains = ahead
+            current = ahead
             if b + AHEAD < B:
                 quantise_x(b + AHEAD)
             if b + 1 < B:
                 ahead = multiply(b + 1)
-            results = [work.tile([P, GROUP, PIX], F32, name="res") for chain in chains]
-            other_terms([chain + (res,) for chain, res in zip(chains, results)])
-            for grp, res in enumerate(results):
-                store(b, grp, res)
+            if by_matrix(b):
+                finish_by_matrix(b, current)
+            else:
+                finish_direct(b, current)

@@ -26,7 +26,6 @@ TERMS = len(OFFSETS)
 REACH = 4
 GROUP = 4
 GROUPS = D_TILES // GROUP
-AHEAD = 2
 
 FLOPS = 2 * B * C * C * PIX + 2 * TERMS * B * C * PIX
 
@@ -44,6 +43,7 @@ def tile_graphaugmentation_pa_kernel(tc, x, mw, mb, attn_w, out):
         stage = stack.enter_context(tc.tile_pool(name="stage", bufs=2))
         work = stack.enter_context(tc.tile_pool(name="work", bufs=4))
         psum = stack.enter_context(tc.psum_pool(name="psum", bufs=8))
+        stack.enter_context(tc.manual_schedule())
 
         x_raw = [keep.tile([P, PASSES * PACK * PIX], BF16, name="x_raw%d" % b) for b in range(B)]
         mw_raw = keep.tile([P, D_TILES, C], BF16)
@@ -55,10 +55,10 @@ def tile_graphaugmentation_pa_kernel(tc, x, mw, mb, attn_w, out):
             )
 
         w_bf = const.tile([P, TERMS * B], BF16)
-        nc.scalar.dma_start(out=w_bf[:], in_=attn_w.rearrange("i b -> (i b)").partition_broadcast(P))
+        nc.sync.dma_start(out=w_bf[:], in_=attn_w.rearrange("i b -> (i b)").partition_broadcast(P))
         mb_rows = const.tile([P, P], BF16)
         nc.vector.memset(mb_rows[:], 0.0)
-        nc.scalar.dma_start(out=mb_rows[0:D_TILES, :], in_=mb.rearrange("(t p) -> t p", p=P))
+        nc.sync.dma_start(out=mb_rows[0:D_TILES, :], in_=mb.rearrange("(t p) -> t p", p=P))
 
         load_x(0)
         for pair in range(D_TILES // 2):
@@ -73,6 +73,11 @@ def tile_graphaugmentation_pa_kernel(tc, x, mw, mb, attn_w, out):
         make_identity(nc, ident[:])
         w_f32 = const.tile([P, TERMS * B], F32)
         nc.vector.tensor_copy(out=w_f32[:], in_=w_bf[:])
+
+        mb_rows_f32 = const.tile([P, P], F32)
+        nc.vector.tensor_copy(out=mb_rows_f32[:], in_=mb_rows[:])
+        mb_t = psum.tile([P, BANK], F32, tag="bank")
+        nc.tensor.transpose(mb_t[:, 0:P], mb_rows_f32[:], ident[:])
 
         def weight(i, b):
             return w_f32[:, i * B + b : i * B + b + 1]
@@ -120,12 +125,9 @@ def tile_graphaugmentation_pa_kernel(tc, x, mw, mb, attn_w, out):
                     scalar1=(-0.5 if over_the_edge and sign == 1 else 0.5),
                 )
         matrix = dict((b, const.tile([P, 2, P], F32, name="matrix%d" % b)) for b in matrix_images)
-        other_terms([first_term(fold_ring, HALF_ROWS, 2, b) + (matrix[b],) for b in matrix_images])
+        matrix_chains = [first_term(fold_ring, HALF_ROWS, 2, b) + (matrix[b],) for b in matrix_images]
+        other_terms(matrix_chains[:2])
 
-        mb_rows_f32 = const.tile([P, P], F32)
-        nc.vector.tensor_copy(out=mb_rows_f32[:], in_=mb_rows[:])
-        mb_t = psum.tile([P, BANK], F32, tag="bank")
-        nc.tensor.transpose(mb_t[:, 0:P], mb_rows_f32[:], ident[:])
         mb_sb = const.tile([P, D_TILES], F32)
         nc.vector.tensor_copy(out=mb_sb[:], in_=mb_t[:, 0:D_TILES])
         w_sum = const.tile([P, B], F32)
@@ -133,6 +135,46 @@ def tile_graphaugmentation_pa_kernel(tc, x, mw, mb, attn_w, out):
         mb_w = dict((b, const.tile([P, D_TILES], F32, name="mb_w%d" % b)) for b in matrix_images)
         for b in matrix_images:
             nc.vector.tensor_scalar_mul(out=mb_w[b][:], in0=mb_sb[:], scalar1=w_sum[:, b : b + 1])
+
+        x_codes = [keep.tile([P, PASSES, PIX], U32, name="x_codes%d" % b, align_bytes=64) for b in range(B)]
+        x_scales = [keep.tile([P, PASSES, PIX], U8, name="x_scales%d" % b, align_bytes=64) for b in range(B)]
+        minus_codes = dict((b, keep.tile([P, PASSES, P], U32, name="minus_codes%d" % b, align_bytes=64)) for b in matrix_images)
+        minus_scales = dict((b, keep.tile([P, PASSES, P], U8, name="minus_scales%d" % b, align_bytes=64)) for b in matrix_images)
+
+        grouped = dict()
+
+        def regroup_x(b):
+            on_vector = b < B - 2
+            rows_of_words = x_raw[b][:].rearrange("q (g t c) -> q g t c", g=PASSES, t=PACK)
+            x_grp = stage.tile([P, PASSES, PIX * PACK], BF16, align_bytes=64)
+            copy = nc.vector.tensor_copy if on_vector else nc.scalar.copy
+            for g in range(PASSES):
+                copy(
+                    out=x_grp[:, g, :].rearrange("q (c i t) -> q c t i", i=4, t=PACK),
+                    in_=rows_of_words[:, g, :, :].rearrange("q t (c i) -> q c t i", i=4),
+                )
+            grouped[b] = [(x_grp, x_codes[b], x_scales[b])]
+            if by_matrix(b):
+                minus_grp = stage.tile([P, PASSES, P * PACK], BF16, align_bytes=64)
+                for g in range(PASSES):
+                    to = minus_grp[:, g, :].rearrange("q (c i t) -> q c t i", i=4, t=PACK)
+                    upper = rows_of_words[:, g, :, P : 2 * P].rearrange("q t (c i) -> q c t i", i=4)
+                    if on_vector:
+                        nc.vector.tensor_scalar_mul(out=to, in0=upper, scalar1=-1.0)
+                    else:
+                        nc.scalar.mul(out=to, in_=upper, mul=-1.0)
+                grouped[b].append((minus_grp, minus_codes[b], minus_scales[b]))
+
+        def quantise_x(b):
+            for values, codes, scales in grouped[b]:
+                nc.vector.quantize_mx(
+                    out=codes[:].rearrange("q g c -> q (g c)").bitcast(FP8X4),
+                    scales=scales[:].rearrange("q g c -> q (g c)"),
+                    in_=values[:].rearrange("q g c -> q (g c)"),
+                )
+
+        regroup_x(0)
+        quantise_x(0)
 
         mw_codes = keep.tile([P, PASSES, C], U32, align_bytes=64)
         mw_scales = keep.tile([P, PASSES, C], U8, align_bytes=64)
@@ -153,38 +195,8 @@ def tile_graphaugmentation_pa_kernel(tc, x, mw, mb, attn_w, out):
                     in_=mw_grp[:, g * P * PACK : (g + 1) * P * PACK],
                 )
 
-        x_codes = [keep.tile([P, PASSES, PIX], U32, name="x_codes%d" % b, align_bytes=64) for b in range(B)]
-        x_scales = [keep.tile([P, PASSES, PIX], U8, name="x_scales%d" % b, align_bytes=64) for b in range(B)]
-        minus_codes = dict((b, keep.tile([P, PASSES, P], U32, name="minus_codes%d" % b, align_bytes=64)) for b in matrix_images)
-        minus_scales = dict((b, keep.tile([P, PASSES, P], U8, name="minus_scales%d" % b, align_bytes=64)) for b in matrix_images)
-
-        def quantise_x(b):
-            regroup = nc.vector.tensor_copy if b < AHEAD else nc.scalar.copy
-            rows_of_words = x_raw[b][:].rearrange("q (g t c) -> q g t c", g=PASSES, t=PACK)
-            x_grp = stage.tile([P, PASSES, PIX * PACK], BF16, align_bytes=64)
-            for g in range(PASSES):
-                regroup(
-                    out=x_grp[:, g, :].rearrange("q (c i t) -> q c t i", i=4, t=PACK),
-                    in_=rows_of_words[:, g, :, :].rearrange("q t (c i) -> q c t i", i=4),
-                )
-            nc.vector.quantize_mx(
-                out=x_codes[b][:].rearrange("q g c -> q (g c)").bitcast(FP8X4),
-                scales=x_scales[b][:].rearrange("q g c -> q (g c)"),
-                in_=x_grp[:].rearrange("q g c -> q (g c)"),
-            )
-            if by_matrix(b):
-                minus_grp = stage.tile([P, PASSES, P * PACK], BF16, align_bytes=64)
-                for g in range(PASSES):
-                    nc.scalar.mul(
-                        out=minus_grp[:, g, :].rearrange("q (c i t) -> q c t i", i=4, t=PACK),
-                        in_=rows_of_words[:, g, :, P : 2 * P].rearrange("q t (c i) -> q c t i", i=4),
-                        mul=-1.0,
-                    )
-                nc.vector.quantize_mx(
-                    out=minus_codes[b][:].rearrange("q g c -> q (g c)").bitcast(FP8X4),
-                    scales=minus_scales[b][:].rearrange("q g c -> q (g c)"),
-                    in_=minus_grp[:].rearrange("q g c -> q (g c)"),
-                )
+        regroup_x(1)
+        quantise_x(1)
 
         def mw_part(g, channels):
             return (mw_codes[:, g, channels], mw_scales[:, g, channels])
@@ -243,7 +255,7 @@ def tile_graphaugmentation_pa_kernel(tc, x, mw, mb, attn_w, out):
             for grp, res in enumerate(results):
                 store(b, grp, res)
 
-        def multiply_by_matrix(b):
+        def multiply_folded(b):
             folded = work.tile([P, 2, C], F32, name="folded", bufs=2)
             for sign in range(2):
                 for n in range(C // BANK):
@@ -256,6 +268,9 @@ def tile_graphaugmentation_pa_kernel(tc, x, mw, mb, attn_w, out):
                     ]
                     mx_group(bank[:], lower + upper)
                     nc.scalar.copy(out=folded[:, sign, channels], in_=bank[:])
+            return folded
+
+        def apply_matrices(b, folded):
             parts = []
             for grp in range(GROUPS):
                 bank_u = psum.tile([P, BANK], F32, tag="bank")
@@ -298,18 +313,25 @@ def tile_graphaugmentation_pa_kernel(tc, x, mw, mb, attn_w, out):
                 store(b, grp, res)
 
         def multiply(b):
-            return multiply_by_matrix(b) if by_matrix(b) else multiply_direct(b)
+            return multiply_folded(b) if by_matrix(b) else multiply_direct(b)
 
-        for b in range(AHEAD):
+        products = dict()
+        products[0] = multiply(0)
+        other_terms(matrix_chains[2:])
+        for b in (2, 3):
+            regroup_x(b)
             quantise_x(b)
-        ahead = multiply(0)
+        products[1] = multiply(1)
         for b in range(B):
-            current = ahead
-            if b + AHEAD < B:
-                quantise_x(b + AHEAD)
-            if b + 1 < B:
-                ahead = multiply(b + 1)
+            if b + 4 < B:
+                regroup_x(b + 4)
+            if b + 2 < B:
+                products[b + 2] = multiply(b + 2)
+            if b + 1 < B and by_matrix(b + 1):
+                products[b + 1] = apply_matrices(b + 1, products[b + 1])
             if by_matrix(b):
-                finish_by_matrix(b, current)
+                finish_by_matrix(b, products[b])
             else:
-                finish_direct(b, current)
+                finish_direct(b, products[b])
+            if b + 4 < B:
+                quantise_x(b + 4)

from contextlib import ExitStack

from concourse import mybir
from concourse.masks import make_identity

F32 = mybir.dt.float32
BF16 = mybir.dt.bfloat16
U32 = mybir.dt.uint32
U8 = mybir.dt.uint8
FP8X4 = mybir.dt.float8_e4m3fn_x4
ACT = mybir.ActivationFunctionType
ALU = mybir.AluOpType

P = 128
PACK = 4
K_PASS = P * PACK
BANK = 512

B, C, H, W = 6, 1024, 16, 16
PIX = H * W
HALF_ROWS = H // 2
PASSES = C // K_PASS
D_TILES = C // P
OFFSETS = [(-4, -4), (-4, -1), (-4, 2), (-3, 4), (-2, -3), (2, 3), (3, -2), (4, 4)]
TERMS = len(OFFSETS)
REACH = 4
GROUP = 4
GROUPS = D_TILES // GROUP

FLOPS = 2 * B * C * C * PIX + 2 * TERMS * B * C * PIX


def by_matrix(b):
    return b % 3 != 0


def tile_graphaugmentation_pa_kernel(tc, x, mw, mb, attn_w, out):
    nc = tc.nc
    matrix_images = [b for b in range(B) if by_matrix(b)]
    with ExitStack() as stack:
        const = stack.enter_context(tc.tile_pool(name="const", bufs=1))
        keep = stack.enter_context(tc.tile_pool(name="keep", bufs=1))
        stage = stack.enter_context(tc.tile_pool(name="stage", bufs=2))
        work = stack.enter_context(tc.tile_pool(name="work", bufs=4))
        psum = stack.enter_context(tc.psum_pool(name="psum", bufs=8))
        stack.enter_context(tc.manual_schedule())

        x_raw = [keep.tile([P, PASSES * PACK * PIX], BF16, name="x_raw%d" % b) for b in range(B)]
        mw_raw = keep.tile([P, D_TILES, C], BF16)

        def load_x(b):
            nc.sync.dma_start(
                out=x_raw[b][:].rearrange("q (s r) -> q s r", s=PASSES * 2),
                in_=x[b].rearrange("(s q e) h w -> q s (e h w)", q=P, e=2),
            )

        w_bf = const.tile([P, TERMS * B], BF16)
        nc.sync.dma_start(out=w_bf[:], in_=attn_w.rearrange("i b -> (i b)").partition_broadcast(P))
        mb_rows = const.tile([P, P], BF16)
        nc.vector.memset(mb_rows[:], 0.0)
        nc.sync.dma_start(out=mb_rows[0:D_TILES, :], in_=mb.rearrange("(t p) -> t p", p=P))

        load_x(0)
        for pair in range(D_TILES // 2):
            nc.sync.dma_start(
                out=mw_raw[:, 2 * pair : 2 * pair + 2, :],
                in_=mw[2 * pair * P : (2 * pair + 2) * P, :].rearrange("(t p) c -> p t c", p=P),
            )
        for b in range(1, B):
            load_x(b)

        ident = const.tile([P, P], F32)
        make_identity(nc, ident[:])
        w_f32 = const.tile([P, TERMS * B], F32)
        nc.vector.tensor_copy(out=w_f32[:], in_=w_bf[:])

        mb_rows_f32 = const.tile([P, P], F32)
        nc.vector.tensor_copy(out=mb_rows_f32[:], in_=mb_rows[:])
        mb_t = psum.tile([P, BANK], F32, tag="bank")
        nc.tensor.transpose(mb_t[:, 0:P], mb_rows_f32[:], ident[:])

        def weight(i, b):
            return w_f32[:, i * B + b : i * B + b + 1]

        def shifted(ring, i, rows):
            dy, dx = OFFSETS[i]
            return ring[:, REACH - dy : REACH - dy + rows, :, (-dx) % W : (-dx) % W + W]

        def first_term(ring, rows, n, b):
            acc = work.tile([P, rows, n, W], F32, name="acc%dx%d" % (rows, n))
            nc.scalar.activation(out=acc[:], in_=shifted(ring, 0, rows), func=ACT.Copy, scale=weight(0, b))
            return (ring, rows, n, b, acc)

        def other_terms(chains):
            for i in range(1, TERMS - 1):
                for ring, rows, n, b, acc, res in chains:
                    nc.vector.scalar_tensor_tensor(
                        out=acc[:], in0=shifted(ring, i, rows), scalar=weight(i, b), in1=acc[:],
                        op0=ALU.mult, op1=ALU.add,
                    )
            for ring, rows, n, b, acc, res in chains:
                for j in range(n):
                    nc.vector.scalar_tensor_tensor(
                        out=res[:, j, :].rearrange("p (h w) -> p h w", w=W),
                        in0=shifted(ring, TERMS - 1, rows)[:, :, j, :],
                        scalar=weight(TERMS - 1, b),
                        in1=acc[:, :, j, :],
                        op0=ALU.mult,
                        op1=ALU.add,
                    )

        fold_ring = const.tile([P, HALF_ROWS + 2 * REACH, 2, 2 * W], F32)
        for ring_row, image_row, n, over_the_edge in [
            (0, HALF_ROWS - REACH, REACH, True),
            (REACH, 0, HALF_ROWS, False),
            (REACH + HALF_ROWS, 0, REACH, True),
        ]:
            for sign in range(2):
                nc.vector.tensor_scalar_mul(
                    out=fold_ring[:, ring_row : ring_row + n, sign, :].rearrange("p r (c w) -> p r c w", c=2),
                    in0=ident[:, image_row * W : (image_row + n) * W]
                    .rearrange("p (r w) -> p r w", w=W)
                    .unsqueeze(2)
                    .to_broadcast([P, n, 2, W]),
                    scalar1=(-0.5 if over_the_edge and sign == 1 else 0.5),
                )
        matrix = dict((b, const.tile([P, 2, P], F32, name="matrix%d" % b)) for b in matrix_images)
        matrix_chains = [first_term(fold_ring, HALF_ROWS, 2, b) + (matrix[b],) for b in matrix_images]
        other_terms(matrix_chains[:2])

        mb_sb = const.tile([P, D_TILES], F32)
        nc.vector.tensor_copy(out=mb_sb[:], in_=mb_t[:, 0:D_TILES])
        w_sum = const.tile([P, B], F32)
        nc.vector.reduce_sum(out=w_sum[:], in_=w_f32[:].rearrange("p (i b) -> p b i", b=B), axis=mybir.AxisListType.X)
        mb_w = dict((b, const.tile([P, D_TILES], F32, name="mb_w%d" % b)) for b in matrix_images)
        for b in matrix_images:
            nc.vector.tensor_scalar_mul(out=mb_w[b][:], in0=mb_sb[:], scalar1=w_sum[:, b : b + 1])

        x_codes = [keep.tile([P, PASSES, PIX], U32, name="x_codes%d" % b, align_bytes=64) for b in range(B)]
        x_scales = [keep.tile([P, PASSES, PIX], U8, name="x_scales%d" % b, align_bytes=64) for b in range(B)]
        minus_codes = dict((b, keep.tile([P, PASSES, P], U32, name="minus_codes%d" % b, align_bytes=64)) for b in matrix_images)
        minus_scales = dict((b, keep.tile([P, PASSES, P], U8, name="minus_scales%d" % b, align_bytes=64)) for b in matrix_images)

        grouped = dict()

        def regroup_x(b):
            on_vector = b < B - 2
            rows_of_words = x_raw[b][:].rearrange("q (g t c) -> q g t c", g=PASSES, t=PACK)
            x_grp = stage.tile([P, PASSES, PIX * PACK], BF16, align_bytes=64)
            copy = nc.vector.tensor_copy if on_vector else nc.scalar.copy
            for g in range(PASSES):
                copy(
                    out=x_grp[:, g, :].rearrange("q (c i t) -> q c t i", i=4, t=PACK),
                    in_=rows_of_words[:, g, :, :].rearrange("q t (c i) -> q c t i", i=4),
                )
            grouped[b] = [(x_grp, x_codes[b], x_scales[b])]
            if by_matrix(b):
                minus_grp = stage.tile([P, PASSES, P * PACK], BF16, align_bytes=64)
                for g in range(PASSES):
                    to = minus_grp[:, g, :].rearrange("q (c i t) -> q c t i", i=4, t=PACK)
                    upper = rows_of_words[:, g, :, P : 2 * P].rearrange("q t (c i) -> q c t i", i=4)
                    if on_vector:
                        nc.vector.tensor_scalar_mul(out=to, in0=upper, scalar1=-1.0)
                    else:
                        nc.scalar.mul(out=to, in_=upper, mul=-1.0)
                grouped[b].append((minus_grp, minus_codes[b], minus_scales[b]))

        def quantise_x(b):
            for values, codes, scales in grouped[b]:
                nc.vector.quantize_mx(
                    out=codes[:].rearrange("q g c -> q (g c)").bitcast(FP8X4),
                    scales=scales[:].rearrange("q g c -> q (g c)"),
                    in_=values[:].rearrange("q g c -> q (g c)"),
                )

        regroup_x(0)
        quantise_x(0)

        mw_codes = keep.tile([P, PASSES, C], U32, align_bytes=64)
        mw_scales = keep.tile([P, PASSES, C], U8, align_bytes=64)
        for t in range(D_TILES):
            words = mw_raw[:, t, :].bitcast(F32)
            w_t = psum.tile([P, BANK], F32, tag="bank")
            for s in range(PASSES * 2):
                nc.tensor.transpose(w_t[:, s * P : (s + 1) * P], words[:, s * P : (s + 1) * P], ident[:])
            mw_grp = stage.tile([P, PASSES * P * PACK], BF16, align_bytes=64)
            nc.scalar.copy(
                out=mw_grp[:].bitcast(F32).rearrange("q (g d u) -> q g d u", g=PASSES, u=2),
                in_=w_t[:].rearrange("q (g u d) -> q g d u", g=PASSES, u=2),
            )
            for g in range(PASSES):
                nc.vector.quantize_mx(
                    out=mw_codes[:, g, t * P : (t + 1) * P].bitcast(FP8X4),
                    scales=mw_scales[:, g, t * P : (t + 1) * P],
                    in_=mw_grp[:, g * P * PACK : (g + 1) * P * PACK],
                )

        regroup_x(1)
        quantise_x(1)

        def mw_part(g, channels):
            return (mw_codes[:, g, channels], mw_scales[:, g, channels])

        def x_part(b, g, pixels):
            return (x_codes[b][:, g, pixels], x_scales[b][:, g, pixels])

        def minus_part(b, g):
            return (minus_codes[b][:, g, :], minus_scales[b][:, g, :])

        def mx_group(acc, pairs):
            for k, (still, moving) in enumerate(pairs):
                nc.tensor.matmul_mx(
                    out=acc,
                    lhsT=still[0].bitcast(FP8X4),
                    lhsT_scale=still[1],
                    rhs=moving[0].bitcast(FP8X4),
                    rhs_scale=moving[1],
                    start=(k == 0),
                    stop=(k == len(pairs) - 1),
                )

        def store(b, grp, res):
            nc.sync.dma_start(
                out=out[b, grp * GROUP * P : (grp + 1) * GROUP * P].rearrange("(j p) h w -> p j (h w)", p=P),
                in_=res[:],
            )

        def multiply_direct(b):
            chains = []
            for grp in range(GROUPS):
                ring = work.tile([P, H + 2 * REACH, GROUP, 2 * W], F32, name="ring")
                for j in range(GROUP):
                    t = grp * GROUP + j
                    channels = slice(t * P, (t + 1) * P)
                    bank = psum.tile([P, BANK], F32, tag="bank")
                    for at, first, n in [(0, PIX // 2, PIX // 2), (PIX // 2, 0, PIX), (PIX // 2 + PIX, 0, PIX // 2)]:
                        mx_group(
                            bank[:, at : at + n],
                            [(mw_part(g, channels), x_part(b, g, slice(first, first + n))) for g in range(PASSES)],
                        )
                    rows = bank[:, (HALF_ROWS - REACH) * W : (HALF_ROWS + H + REACH) * W]
                    nc.scalar.activation(
                        out=ring[:, :, j, :].rearrange("p r (c w) -> p r c w", c=2),
                        in_=rows.rearrange("p (r w) -> p r w", w=W).unsqueeze(2).to_broadcast([P, H + 2 * REACH, 2, W]),
                        func=ACT.Identity,
                        bias=mb_sb[:, t : t + 1],
                        scale=1.0,
                    )
                chains.append(first_term(ring, H, GROUP, b))
            return chains

        def finish_direct(b, chains):
            results = [work.tile([P, GROUP, PIX], F32, name="res") for chain in chains]
            other_terms([chain + (res,) for chain, res in zip(chains, results)])
            for grp, res in enumerate(results):
                store(b, grp, res)

        def multiply_folded(b):
            folded = work.tile([P, 2, C], F32, name="folded", bufs=2)
            for sign in range(2):
                for n in range(C // BANK):
                    channels = slice(n * BANK, (n + 1) * BANK)
                    bank = psum.tile([P, BANK], F32, tag="bank")
                    lower = [(x_part(b, g, slice(0, P)), mw_part(g, channels)) for g in range(PASSES)]
                    upper = [
                        (x_part(b, g, slice(P, 2 * P)) if sign == 0 else minus_part(b, g), mw_part(g, channels))
                        for g in range(PASSES)
                    ]
                    mx_group(bank[:], lower + upper)
                    nc.scalar.copy(out=folded[:, sign, channels], in_=bank[:])
            return folded

        def apply_matrices(b, folded):
            parts = []
            for grp in range(GROUPS):
                bank_u = psum.tile([P, BANK], F32, tag="bank")
                bank_v = psum.tile([P, BANK], F32, tag="bank")
                for sign, bank in enumerate((bank_u, bank_v)):
                    for j in range(GROUP):
                        t = grp * GROUP + j
                        nc.tensor.matmul(
                            out=bank[:, j * P : (j + 1) * P],
                            lhsT=folded[:, sign, t * P : (t + 1) * P],
                            rhs=matrix[b][:, sign, :],
                            start=True,
                            stop=True,
                        )
                u_sb = work.tile([P, GROUP, P], F32, name="u_sb")
                for j in range(GROUP):
                    t = grp * GROUP + j
                    nc.scalar.activation(
                        out=u_sb[:, j, :],
                        in_=bank_u[:, j * P : (j + 1) * P],
                        func=ACT.Identity,
                        bias=mb_w[b][:, t : t + 1],
                        scale=1.0,
                    )
                parts.append((u_sb, bank_v))
            return parts

        def finish_by_matrix(b, parts):
            for grp, (u_sb, bank_v) in enumerate(parts):
                res = work.tile([P, GROUP, PIX], F32, name="res")
                for half, sign in enumerate((1.0, -1.0)):
                    nc.vector.scalar_tensor_tensor(
                        out=res[:, :, half * P : (half + 1) * P],
                        in0=bank_v[:].rearrange("p (j c) -> p j c", j=GROUP),
                        scalar=sign,
                        in1=u_sb[:],
                        op0=ALU.mult,
                        op1=ALU.add,
                    )
                store(b, grp, res)

        def multiply(b):
            return multiply_folded(b) if by_matrix(b) else multiply_direct(b)

        products = dict()
        products[0] = multiply(0)
        other_terms(matrix_chains[2:])
        for b in (2, 3):
            regroup_x(b)
            quantise_x(b)
        products[1] = multiply(1)
        for b in range(B):
            if b + 4 < B:
                regroup_x(b + 4)
            if b + 2 < B:
                products[b + 2] = multiply(b + 2)
            if b + 1 < B and by_matrix(b + 1):
                products[b + 1] = apply_matrices(b + 1, products[b + 1])
            if by_matrix(b):
                finish_by_matrix(b, products[b])
            else:
                finish_direct(b, products[b])
            if b + 4 < B:
                quantise_x(b + 4)
